import numpy as np
import ml_dtypes


def mxq(x, axis, fmt="e4m3"):
    dtype, down = {"e4m3": (ml_dtypes.float8_e4m3fn, 7), "e5m2": (ml_dtypes.float8_e5m2, 14)}[fmt]
    v = np.moveaxis(np.asarray(x, np.float32).astype(ml_dtypes.bfloat16).astype(np.float64), axis, -1)
    blocks = v.reshape(v.shape[:-1] + (-1, 32))
    amax = np.abs(blocks).max(-1, keepdims=True)
    byte = np.maximum(np.where(amax > 0, np.frexp(amax)[1] - 1 + 127, 0) - down, 1)
    scale = np.exp2(byte - 127.0)
    codes = (blocks / scale).astype(np.float32).astype(dtype).astype(np.float64)
    return np.moveaxis((codes * scale).reshape(v.shape), -1, axis)


WIDE = False


def mx_kscale(k):
    if not WIDE:
        return np.ones(k)
    levels = np.array([30, -30])
    if k % 512:
        return np.exp2(np.random.permutation(np.resize(levels, k // 32))).repeat(32)
    a = np.empty((k // 512, 16))
    for p in range(k // 512):
        a[p, :8] = np.random.permutation(np.resize(levels, 8))
        for g in range(8):
            far = levels[np.abs(levels - a[p, g]) >= 10]
            a[p, g + 8] = far[np.random.randint(len(far))]
    return np.exp2(a.ravel()).repeat(32)


BF16 = ml_dtypes.bfloat16


def bf(x):
    return np.asarray(x, np.float32).astype(BF16)


def f64(x):
    return np.asarray(x).astype(np.float64)


B, S, D, HD, M = 4, 1024, 2048, 128, 4
N = S // M
NEG = float(np.finfo(np.float32).min)


def prev(x):
    return np.concatenate([np.zeros_like(x[:, :1]), x[:, :-1]], axis=1)


def setup_inputs():
    s = mx_kscale(D)

    def w():
        return bf(np.random.standard_normal((D, HD)) / np.sqrt(D) / s[:, None])

    return {"h": bf(np.random.standard_normal((B, S, D)) * s),
            "w_kv_a": w(), "w_kv_b": w(), "w_z_a": w(), "w_z_b": w(),
            "b_a": bf(np.random.standard_normal((M, HD)) * 0.5),
            "b_b": bf(np.random.standard_normal((M, HD)) * 0.5)}


def reference(h, w_kv_a, w_kv_b, w_z_a, w_z_b, b_a, b_b):
    hq = mxq(f64(h), 2, "e5m2")
    c_a = (hq @ mxq(f64(w_kv_a), 0, "e4m3")).reshape(B, N, M, HD)
    c_b = (hq @ mxq(f64(w_kv_b), 0, "e4m3")).reshape(B, N, M, HD)
    z_a = (hq @ mxq(f64(w_z_a), 0, "e4m3")).reshape(B, N, M, HD)
    z_b = (hq @ mxq(f64(w_z_b), 0, "e4m3")).reshape(B, N, M, HD)
    logits = np.concatenate([prev(z_b) + f64(b_b), z_a + f64(b_a)], axis=2)
    valid = np.concatenate([np.broadcast_to((np.arange(N) > 0)[:, None], (N, M)), np.ones((N, M), bool)], axis=1)
    logits = np.where(valid[None, :, :, None], logits, NEG)
    e = np.exp(logits - logits.max(axis=2, keepdims=True))
    weights = e / e.sum(axis=2, keepdims=True)
    c_vals = np.concatenate([prev(c_b), c_a], axis=2)
    return np.sum(weights * c_vals, axis=2)

@@ -1,0 +1,351 @@
+from contextlib import ExitStack
+
+import concourse.mybir as mybir
+from concourse.masks import make_identity
+
+F32 = mybir.dt.float32
+BF16 = mybir.dt.bfloat16
+U32 = mybir.dt.uint32
+U8 = mybir.dt.uint8
+E4M3X4 = mybir.dt.float8_e4m3fn_x4
+E5M2X4 = mybir.dt.float8_e5m2_x4
+ALU = mybir.AluOpType
+ACT = mybir.ActivationFunctionType
+
+B, S, D, HD, M = 4, 1024, 2048, 128, 4
+P = 128
+K_PASS = 512
+PASSES = D // K_PASS
+TOK = P * M
+GROUPS = B * S // TOK
+BLOCKS = S // M
+L_COLS = BLOCKS + 8
+NEG = -(2.0 - 2.0 ** -23) * 2.0 ** 127
+H_BUFS = 8
+
+FLOPS = 2 * B * S * D * 4 * HD
+
+
+def tile_tokenlevelcompressor_pa_kernel(tc, h, w_kv_a, w_kv_b, w_z_a, w_z_b, b_a, b_b, out):
+    nc = tc.nc
+    h_rows = h.flatten_outer_dims()
+    out_rows = out.flatten_outer_dims()
+
+    with ExitStack() as ctx:
+        keep = ctx.enter_context(tc.tile_pool(name="keep", bufs=1))
+        stream = ctx.enter_context(tc.tile_pool(name="stream", bufs=2))
+        psum = ctx.enter_context(tc.psum_pool(name="psum", bufs=1))
+        ctx.enter_context(tc.manual_schedule())
+
+        ident = keep.tile([P, P], F32, name="ident")
+        bias_rows = keep.tile([2 * M, HD], BF16, name="bias_rows")
+        bias_sq = keep.tile([P, P], F32, name="bias_sq")
+        bias = keep.tile([P, 2 * M], F32, name="bias")
+        logits = [keep.tile([P, 2 * M, L_COLS], F32, name="logits%d" % s) for s in range(2)]
+        terms = [keep.tile([P, 2, 2 * M, P], F32, name="terms%d" % s) for s in range(2)]
+        carry = keep.tile([P, M, 1], F32, name="carry")
+        weights = {"za": w_z_a, "zb": w_z_b, "ca": w_kv_a, "cb": w_kv_b}
+        w_raw, w_codes, w_scales = {}, {}, {}
+        for key in weights:
+            w_raw[key] = keep.tile([P, PASSES, M, HD], BF16, name="w_raw_" + key)
+            w_codes[key] = keep.tile([P, PASSES * HD], U32, name="w_codes_" + key, align_bytes=64)
+            w_scales[key] = keep.tile([P, PASSES * HD], U8, name="w_scales_" + key, align_bytes=64)
+
+        h_raw, h_side, h_codes, h_scales, acc, result = {}, {}, {}, {}, {}, {}
+        state = {}
+
+        def load_h(n, first=0, last=2):
+            g, half = divmod(n, 2)
+            if first == 0:
+                h_raw[n] = stream.tile([P, M, 2 * K_PASS], BF16, name="h_raw", bufs=H_BUFS)
+            rows = h_rows[g * TOK : (g + 1) * TOK, half * 2 * K_PASS : (half + 1) * 2 * K_PASS]
+            cols = slice(first * K_PASS, last * K_PASS)
+            nc.sync.dma_start(out=h_raw[n][:, :, cols], in_=rows.rearrange("(j i) k -> j i k", i=M)[:, :, cols])
+
+        def load_w(key):
+            nc.sync.dma_start(out=w_raw[key][:], in_=weights[key].rearrange("(g p t) c -> p g t c", p=P, t=4))
+
+        def interleave_w(key):
+            side = stream.tile([P, PASSES, HD, 4], BF16, name="w_side", align_bytes=64)
+            for g in range(PASSES):
+                nc.vector.tensor_copy(
+                    out=side[:, g].rearrange("p (c i) t -> p c t i", i=4),
+                    in_=w_raw[key][:, g].rearrange("p t (c i) -> p c t i", i=4),
+                )
+            state["side", key] = side
+
+        def quantize_w(key):
+            nc.vector.quantize_mx(
+                out=w_codes[key][:].bitcast(E4M3X4),
+                scales=w_scales[key][:],
+                in_=state["side", key][:].rearrange("p g c t -> p (g c t)"),
+            )
+
+        def transpose_h(n, first=0, last=2):
+            words = h_raw[n][:].rearrange("p i k -> p (i k)").bitcast(F32)
+            if first == 0:
+                h_side[n] = stream.tile([P, 2 * TOK * 4], BF16, name="h_side", bufs=3, align_bytes=64)
+            side_words = h_side[n][:].bitcast(F32)
+            for q in range(first, last):
+                for pair in range(2):
+                    bank = psum.tile([P, 2, 2, P], F32, name="turned", bufs=4)
+                    for ii in range(2):
+                        base = (2 * pair + ii) * K_PASS + q * 256
+                        for u in range(2):
+                            nc.tensor.transpose(bank[:, ii, u, :], words[:, base + u : base + 256 : 2], ident[:])
+                    at = q * 1024 + pair * 512
+                    nc.scalar.copy(
+                        out=side_words[:, at : at + 512].rearrange("p (i r u) -> p i r u", i=2, u=2),
+                        in_=bank[:].rearrange("p i u r -> p i r u"),
+                    )
+
+        def quantize_h(n, first=0, last=2):
+            if first == 0:
+                h_codes[n] = stream.tile([P, 2 * TOK], U32, name="h_codes", bufs=4, align_bytes=64)
+                h_scales[n] = stream.tile([P, 2 * TOK], U8, name="h_scales", bufs=4, align_bytes=64)
+            cols = slice(first * TOK, last * TOK)
+            nc.vector.quantize_mx(
+                out=h_codes[n][:, cols].bitcast(E5M2X4),
+                scales=h_scales[n][:, cols],
+                in_=h_side[n][:, first * TOK * 4 : last * TOK * 4],
+            )
+
+        def project(g, key, first=0, last=PASSES):
+            if first == 0:
+                acc[key] = psum.tile([P, M, P], F32, name="acc_" + key)
+            for k in range(first, last):
+                n, q = 2 * g + k // 2, k % 2
+                w_cols = slice(k * HD, (k + 1) * HD)
+                h_cols = slice(q * TOK, (q + 1) * TOK)
+                nc.tensor.matmul_mx(
+                    out=acc[key][:].rearrange("p i j -> p (i j)"),
+                    lhsT=w_codes[key][:, w_cols].bitcast(E4M3X4),
+                    lhsT_scale=w_scales[key][:, w_cols],
+                    rhs=h_codes[n][:, h_cols].bitcast(E5M2X4),
+                    rhs_scale=h_scales[n][:, h_cols],
+                    start=(k == 0),
+                    stop=(k == PASSES - 1),
+                )
+
+        def add_bias(g, key):
+            seq, half = divmod(g, 2)
+            entry0, col0 = (0, half * P + 1) if key == "zb" else (M, half * P)
+            for i in range(M):
+                e = entry0 + i
+                nc.scalar.activation(
+                    out=logits[seq % 2][:, e, col0 : col0 + P],
+                    in_=acc[key][:, i, :],
+                    func=ACT.Identity,
+                    bias=bias[:, e : e + 1],
+                )
+
+        def window(g):
+            seq, half = divmod(g, 2)
+            return logits[seq % 2][:, :, half * P : (half + 1) * P]
+
+        def max4(g):
+            t = stream.tile([P, 4, P], F32, name="max4")
+            nc.vector.tensor_tensor(out=t[:], in0=window(g)[:, 0:4, :], in1=window(g)[:, 4:8, :], op=ALU.max)
+            state["max4"] = t
+
+        def max2(g):
+            t = stream.tile([P, 2, P], F32, name="max2")
+            nc.vector.tensor_tensor(out=t[:], in0=state["max4"][:, 0:2, :], in1=state["max4"][:, 2:4, :], op=ALU.max)
+            state["max2"] = t
+
+        def max1(g):
+            t = stream.tile([P, 1, P], F32, name="max1")
+            nc.vector.tensor_tensor(out=t[:], in0=state["max2"][:, 0:1, :], in1=state["max2"][:, 1:2, :], op=ALU.max)
+            state["max1"] = t
+
+        def shift(g, first=0, last=2 * M):
+            if first == 0:
+                state["shifted"] = stream.tile([P, 2 * M, P], F32, name="shifted")
+            nc.vector.tensor_tensor(
+                out=state["shifted"][:, first:last, :],
+                in0=window(g)[:, first:last, :],
+                in1=state["max1"][:].to_broadcast([P, last - first, P]),
+                op=ALU.subtract,
+            )
+
+        def exponentiate(g, first=0, last=2 * M):
+            nc.scalar.activation(
+                out=terms[g % 2][:, 0, first:last, :], in_=state["shifted"][:, first:last, :], func=ACT.Exp
+            )
+
+        def weigh_b(g):
+            t = terms[g % 2]
+            nc.vector.tensor_tensor(
+                out=t[:, 1, 0:M, 1:P], in0=acc["cb"][:, :, 0 : P - 1], in1=t[:, 0, 0:M, 1:P], op=ALU.mult
+            )
+            if g % 2 == 0:
+                nc.vector.tensor_copy(out=carry[:], in_=acc["cb"][:, :, P - 1 : P])
+            else:
+                nc.vector.tensor_tensor(out=t[:, 1, 0:M, 0:1], in0=carry[:], in1=t[:, 0, 0:M, 0:1], op=ALU.mult)
+
+        def weigh_a(g):
+            t = terms[g % 2]
+            nc.vector.tensor_tensor(out=t[:, 1, M:, :], in0=acc["ca"][:], in1=t[:, 0, M:, :], op=ALU.mult)
+
+        def sum4(g):
+            t = stream.tile([P, 2, 4, P], F32, name="sum4")
+            for s in range(2):
+                nc.vector.tensor_tensor(
+                    out=t[:, s], in0=terms[g % 2][:, s, 0:4, :], in1=terms[g % 2][:, s, 4:8, :], op=ALU.add
+                )
+            state["sum4"] = t
+
+        def sum2(g):
+            t = stream.tile([P, 2, 2, P], F32, name="sum2")
+            s4 = state["sum4"]
+            nc.vector.tensor_tensor(out=t[:], in0=s4[:, :, 0:2, :], in1=s4[:, :, 2:4, :], op=ALU.add)
+            state["sum2"] = t
+
+        def sum1(g):
+            t = stream.tile([P, 2, P], F32, name="sum1")
+            s2 = state["sum2"]
+            nc.vector.tensor_tensor(out=t[:], in0=s2[:, :, 0, :], in1=s2[:, :, 1, :], op=ALU.add)
+            state["sum1"] = t
+
+        def invert(g):
+            t = stream.tile([P, P], F32, name="inverse")
+            nc.vector.reciprocal(out=t[:], in_=state["sum1"][:, 0, :])
+            state["inverse"] = t
+
+        def normalise(g):
+            result[g] = stream.tile([P, P], F32, name="result")
+            nc.vector.tensor_tensor(out=result[g][:], in0=state["sum1"][:, 1, :], in1=state["inverse"][:], op=ALU.mult)
+
+        def emit(g):
+            bank = psum.tile([P, P], F32, name="acc_za")
+            nc.tensor.transpose(bank[:], result[g][:], ident[:])
+            rows = stream.tile([P, HD], F32, name="rows")
+            nc.scalar.copy(out=rows[:], in_=bank[:])
+            nc.sync.dma_start(out=out_rows[g * P : (g + 1) * P, :], in_=rows[:])
+
+        def sum_turned(g, s, bank, first, last):
+            for e in range(first, last):
+                nc.tensor.matmul(
+                    out=bank[:],
+                    lhsT=terms[g % 2][:, s, e, :],
+                    rhs=ident[:],
+                    start=(e == 0),
+                    stop=(e == 2 * M - 1),
+                    is_transpose=True,
+                )
+
+        nc.scalar.dma_start(out=bias_rows[0:M, :], in_=b_b)
+        nc.scalar.dma_start(out=bias_rows[M : 2 * M, :], in_=b_a)
+        load_h(0, 0, 1)
+        load_w("zb")
+        load_h(0, 1, 2)
+        load_w("za")
+        load_h(1, 0, 1)
+        load_h(1, 1, 2)
+        load_h(2)
+        load_w("cb")
+        load_h(3)
+        load_w("ca")
+        for n in range(4, H_BUFS):
+            load_h(n)
+        make_identity(nc, ident[:])
+        nc.gpsimd.memset(bias_sq[:], 0.0)
+        for s in range(2):
+            nc.vector.memset(logits[s][:, 0:M, 0:1], NEG)
+        nc.vector.memset(terms[0][:, 1, 0:M, 0:1], 0.0)
+        nc.scalar.activation(out=bias_sq[0 : 2 * M, :], in_=bias_rows[:], func=ACT.Identity)
+
+        transpose_h(0, 0, 1)
+        bias_bank = psum.tile([P, P], F32, name="acc_ca")
+        nc.tensor.transpose(bias_bank[:], bias_sq[:], ident[:])
+        nc.scalar.copy(out=bias[:], in_=bias_bank[:, 0 : 2 * M])
+        interleave_w("zb")
+        quantize_h(0, 0, 1)
+        quantize_w("zb")
+        transpose_h(0, 1, 2)
+        interleave_w("za")
+        quantize_h(0, 1, 2)
+        quantize_w("za")
+        transpose_h(1, 0, 1)
+        quantize_h(1, 0, 1)
+        project(0, "zb", 0, 1)
+        project(0, "za", 0, 1)
+        transpose_h(1, 1, 2)
+        quantize_h(1, 1, 2)
+        for k in range(1, PASSES):
+            project(0, "zb", k, k + 1)
+            project(0, "za", k, k + 1)
+        add_bias(0, "zb")
+        add_bias(0, "za")
+        transpose_h(2)
+        load_h(H_BUFS)
+        interleave_w("cb")
+        max4(0)
+        quantize_w("cb")
+        max2(0)
+        project(0, "cb")
+        max1(0)
+        quantize_h(2)
+        shift(0)
+        exponentiate(0)
+        transpose_h(3)
+        load_h(H_BUFS + 1)
+        interleave_w("ca")
+        weigh_b(0)
+        quantize_w("ca")
+        project(0, "ca")
+        quantize_h(3)
+        weigh_a(0)
+        sum4(0)
+
+        last = GROUPS - 1
+        for g in range(1, GROUPS):
+            ahead = g < last
+            if g >= 2:
+                emit(g - 2)
+            if ahead:
+                transpose_h(2 * g + 2)
+                if 2 * g + H_BUFS < 2 * GROUPS:
+                    load_h(2 * g + H_BUFS)
+            project(g, "zb")
+            project(g, "za")
+            add_bias(g, "zb")
+            add_bias(g, "za")
+            if ahead:
+                quantize_h(2 * g + 2)
+                transpose_h(2 * g + 3)
+                if 2 * g + H_BUFS + 1 < 2 * GROUPS:
+                    load_h(2 * g + H_BUFS + 1)
+            sum2(g - 1)
+            max4(g)
+            sum1(g - 1)
+            max2(g)
+            invert(g - 1)
+            max1(g)
+            normalise(g - 1)
+            project(g, "cb")
+            project(g, "ca")
+            if ahead:
+                shift(g)
+                exponentiate(g)
+                quantize_h(2 * g + 3)
+                weigh_b(g)
+                weigh_a(g)
+                sum4(g)
+
+        emit(last - 1)
+        denominators = psum.tile([P, P], F32, name="acc_zb")
+        numerators = psum.tile([P, P], F32, name="acc_za")
+        shift(last, 0, M)
+        exponentiate(last, 0, M)
+        shift(last, M, 2 * M)
+        exponentiate(last, M, 2 * M)
+        weigh_b(last)
+        weigh_a(last)
+        sum_turned(last, 0, denominators, 0, 2 * M)
+        sum_turned(last, 1, numerators, 0, 2 * M)
+        inverse = stream.tile([P, P], F32, name="inverse")
+        nc.vector.reciprocal(out=inverse[:], in_=denominators[:])
+        rows = stream.tile([P, HD], F32, name="rows")
+        nc.vector.tensor_tensor(out=rows[:], in0=numerators[:], in1=inverse[:], op=ALU.mult)
+        nc.sync.dma_start(out=out_rows[last * P :, :], in_=rows[:])

@@ -22,6 +22,7 @@ BLOCKS = S // M
 L_COLS = BLOCKS + 8
 NEG = -(2.0 - 2.0 ** -23) * 2.0 ** 127
 H_BUFS = 8
+SORTED = (2, 2)
 
 FLOPS = 2 * B * S * D * 4 * HD
 
@@ -41,7 +42,7 @@ def tile_tokenlevelcompressor_pa_kernel(tc, h, w_kv_a, w_kv_b, w_z_a, w_z_b, b_a
         bias_rows = keep.tile([2 * M, HD], BF16, name="bias_rows")
         bias_sq = keep.tile([P, P], F32, name="bias_sq")
         bias = keep.tile([P, 2 * M], F32, name="bias")
-        logits = [keep.tile([P, 2 * M, L_COLS], F32, name="logits%d" % s) for s in range(2)]
+        logits = [keep.tile([P, M, L_COLS], F32, name="logits%d" % s) for s in range(2)]
         terms = [keep.tile([P, 2, 2 * M, P], F32, name="terms%d" % s) for s in range(2)]
         carry = keep.tile([P, M, 1], F32, name="carry")
         weights = {"za": w_z_a, "zb": w_z_b, "ca": w_kv_a, "cb": w_kv_b}
@@ -51,7 +52,7 @@ def tile_tokenlevelcompressor_pa_kernel(tc, h, w_kv_a, w_kv_b, w_z_a, w_z_b, b_a
             w_codes[key] = keep.tile([P, PASSES * HD], U32, name="w_codes_" + key, align_bytes=64)
             w_scales[key] = keep.tile([P, PASSES * HD], U8, name="w_scales_" + key, align_bytes=64)
 
-        h_raw, h_side, h_codes, h_scales, acc, result = {}, {}, {}, {}, {}, {}
+        h_raw, h_sorted, h_side, h_codes, h_scales, acc, result = {}, {}, {}, {}, {}, {}, {}
         state = {}
 
         def load_h(n, first=0, last=2):
@@ -65,10 +66,10 @@ def tile_tokenlevelcompressor_pa_kernel(tc, h, w_kv_a, w_kv_b, w_z_a, w_z_b, b_a
         def load_w(key):
             nc.sync.dma_start(out=w_raw[key][:], in_=weights[key].rearrange("(g p t) c -> p g t c", p=P, t=4))
 
-        def interleave_w(key):
+        def interleave_w(key, copy=nc.vector.tensor_copy):
             side = stream.tile([P, PASSES, HD, 4], BF16, name="w_side", align_bytes=64)
             for g in range(PASSES):
-                nc.vector.tensor_copy(
+                copy(
                     out=side[:, g].rearrange("p (c i) t -> p c t i", i=4),
                     in_=w_raw[key][:, g].rearrange("p t (c i) -> p c t i", i=4),
                 )
@@ -79,6 +80,18 @@ def tile_tokenlevelcompressor_pa_kernel(tc, h, w_kv_a, w_kv_b, w_z_a, w_z_b, b_a
                 out=w_codes[key][:].bitcast(E4M3X4),
                 scales=w_scales[key][:],
                 in_=state["side", key][:].rearrange("p g c t -> p (g c t)"),
+            )
+
+        def sort_h(n):
+            count = SORTED[n % 2]
+            if count == 0:
+                return
+            words = h_raw[n][:].rearrange("p i k -> p (i k)").bitcast(F32).rearrange("p (i w) -> p i w", i=M)
+            h_sorted[n] = stream.tile([P, M, 2, P], F32, name="h_sorted", bufs=3)
+            first = M - 2 * count
+            nc.scalar.copy(
+                out=h_sorted[n][:, first:],
+                in_=words[:, first:, 256:512].rearrange("p i (r u) -> p i u r", u=2),
             )
 
         def transpose_h(n, first=0, last=2):
@@ -92,7 +105,11 @@ def tile_tokenlevelcompressor_pa_kernel(tc, h, w_kv_a, w_kv_b, w_z_a, w_z_b, b_a
                     for ii in range(2):
                         base = (2 * pair + ii) * K_PASS + q * 256
                         for u in range(2):
-                            nc.tensor.transpose(bank[:, ii, u, :], words[:, base + u : base + 256 : 2], ident[:])
+                            if n in h_sorted and q == 1 and pair >= 2 - SORTED[n % 2]:
+                                source = h_sorted[n][:, 2 * pair + ii, u, :]
+                            else:
+                                source = words[:, base + u : base + 256 : 2]
+                            nc.tensor.transpose(bank[:, ii, u, :], source, ident[:])
                     at = q * 1024 + pair * 512
                     nc.scalar.copy(
                         out=side_words[:, at : at + 512].rearrange("p (i r u) -> p i r u", i=2, u=2),
@@ -127,26 +144,32 @@ def tile_tokenlevelcompressor_pa_kernel(tc, h, w_kv_a, w_kv_b, w_z_a, w_z_b, b_a
                     stop=(k == PASSES - 1),
                 )
 
-        def add_bias(g, key):
+        def add_bias(g):
             seq, half = divmod(g, 2)
-            entry0, col0 = (0, half * P + 1) if key == "zb" else (M, half * P)
             for i in range(M):
-                e = entry0 + i
                 nc.scalar.activation(
-                    out=logits[seq % 2][:, e, col0 : col0 + P],
-                    in_=acc[key][:, i, :],
+                    out=logits[seq % 2][:, i, half * P + 1 : (half + 1) * P + 1],
+                    in_=acc["zb"][:, i, :],
                     func=ACT.Identity,
-                    bias=bias[:, e : e + 1],
+                    bias=bias[:, i : i + 1],
                 )
 
         def window(g):
             seq, half = divmod(g, 2)
             return logits[seq % 2][:, :, half * P : (half + 1) * P]
 
-        def max4(g):
-            t = stream.tile([P, 4, P], F32, name="max4")
-            nc.vector.tensor_tensor(out=t[:], in0=window(g)[:, 0:4, :], in1=window(g)[:, 4:8, :], op=ALU.max)
-            state["max4"] = t
+        def max4(g, first, last):
+            if first == 0:
+                state["max4"] = stream.tile([P, M, P], F32, name="max4")
+            for i in range(first, last):
+                nc.vector.scalar_tensor_tensor(
+                    out=state["max4"][:, i, :],
+                    in0=acc["za"][:, i, :],
+                    scalar=bias[:, M + i : M + i + 1],
+                    in1=window(g)[:, i, :],
+                    op0=ALU.add,
+                    op1=ALU.max,
+                )
 
         def max2(g):
             t = stream.tile([P, 2, P], F32, name="max2")
@@ -158,15 +181,25 @@ def tile_tokenlevelcompressor_pa_kernel(tc, h, w_kv_a, w_kv_b, w_z_a, w_z_b, b_a
             nc.vector.tensor_tensor(out=t[:], in0=state["max2"][:, 0:1, :], in1=state["max2"][:, 1:2, :], op=ALU.max)
             state["max1"] = t
 
-        def shift(g, first=0, last=2 * M):
-            if first == 0:
-                state["shifted"] = stream.tile([P, 2 * M, P], F32, name="shifted")
+        def shift_b(g):
+            state["shifted"] = stream.tile([P, 2 * M, P], F32, name="shifted")
             nc.vector.tensor_tensor(
-                out=state["shifted"][:, first:last, :],
-                in0=window(g)[:, first:last, :],
-                in1=state["max1"][:].to_broadcast([P, last - first, P]),
+                out=state["shifted"][:, 0:M, :],
+                in0=window(g),
+                in1=state["max1"][:].to_broadcast([P, M, P]),
                 op=ALU.subtract,
             )
+
+        def shift_a(g):
+            for i in range(M):
+                nc.vector.scalar_tensor_tensor(
+                    out=state["shifted"][:, M + i, :],
+                    in0=acc["za"][:, i, :],
+                    scalar=bias[:, M + i : M + i + 1],
+                    in1=state["max1"][:, 0, :],
+                    op0=ALU.add,
+                    op1=ALU.subtract,
+                )
 
         def exponentiate(g, first=0, last=2 * M):
             nc.scalar.activation(
@@ -207,17 +240,50 @@ def tile_tokenlevelcompressor_pa_kernel(tc, h, w_kv_a, w_kv_b, w_z_a, w_z_b, b_a
             nc.vector.tensor_tensor(out=t[:], in0=s2[:, :, 0, :], in1=s2[:, :, 1, :], op=ALU.add)
             state["sum1"] = t
 
+        def pair_products(g):
+            t = stream.tile([P, 2, P // 4], F32, name="pairs")
+            den = state["sum1"][:, 0, :]
+            nc.vector.tensor_tensor(
+                out=t[:].rearrange("p a j -> p (a j)"), in0=den[:, 0 : P // 2], in1=den[:, P // 2 :], op=ALU.mult
+            )
+            state["pairs"] = t
+
+        def quad_products(g):
+            t = stream.tile([P, 1, P // 4], F32, name="quads")
+            nc.vector.tensor_tensor(out=t[:], in0=state["pairs"][:, 0:1, :], in1=state["pairs"][:, 1:2, :], op=ALU.mult)
+            state["quads"] = t
+
+        def invert_quads(g):
+            t = stream.tile([P, 1, P // 4], F32, name="quad_inverse")
+            nc.vector.reciprocal(out=t[:], in_=state["quads"][:])
+            state["quad_inverse"] = t
+
+        def invert_pairs(g):
+            t = stream.tile([P, 1, P // 2], F32, name="pair_inverse")
+            nc.vector.tensor_tensor(
+                out=t[:].rearrange("p o (a j) -> p (o a) j", a=2),
+                in0=state["pairs"][:, ::-1, :],
+                in1=state["quad_inverse"][:].to_broadcast([P, 2, P // 4]),
+                op=ALU.mult,
+            )
+            state["pair_inverse"] = t
+
         def invert(g):
             t = stream.tile([P, P], F32, name="inverse")
-            nc.vector.reciprocal(out=t[:], in_=state["sum1"][:, 0, :])
+            nc.vector.tensor_tensor(
+                out=t[:].rearrange("p (a j) -> p a j", a=2),
+                in0=state["sum1"][:, 0, :].rearrange("p (a j) -> p a j", a=2)[:, ::-1, :],
+                in1=state["pair_inverse"][:].to_broadcast([P, 2, P // 2]),
+                op=ALU.mult,
+            )
             state["inverse"] = t
 
         def normalise(g):
             result[g] = stream.tile([P, P], F32, name="result")
             nc.vector.tensor_tensor(out=result[g][:], in0=state["sum1"][:, 1, :], in1=state["inverse"][:], op=ALU.mult)
 
-        def emit(g):
-            bank = psum.tile([P, P], F32, name="acc_za")
+        def emit(g, tag="acc_cb", bufs=1):
+            bank = psum.tile([P, P], F32, name=tag, bufs=bufs)
             nc.tensor.transpose(bank[:], result[g][:], ident[:])
             rows = stream.tile([P, HD], F32, name="rows")
             nc.scalar.copy(out=rows[:], in_=bank[:])
@@ -272,80 +338,116 @@ def tile_tokenlevelcompressor_pa_kernel(tc, h, w_kv_a, w_kv_b, w_z_a, w_z_b, b_a
         project(0, "za", 0, 1)
         transpose_h(1, 1, 2)
         quantize_h(1, 1, 2)
-        for k in range(1, PASSES):
-            project(0, "zb", k, k + 1)
-            project(0, "za", k, k + 1)
-        add_bias(0, "zb")
-        add_bias(0, "za")
+        project(0, "zb", 1, 2)
+        project(0, "za", 1, 2)
+        project(0, "zb", 2, 3)
+        project(0, "za", 2, 3)
+        project(0, "zb", 3, 4)
+        project(0, "za", 3, 4)
+        add_bias(0)
         transpose_h(2)
         load_h(H_BUFS)
         interleave_w("cb")
-        max4(0)
+        max4(0, 0, M)
         quantize_w("cb")
         max2(0)
         project(0, "cb")
         max1(0)
+        interleave_w("ca")
+        shift_b(0)
+        shift_a(0)
+        quantize_w("ca")
         quantize_h(2)
-        shift(0)
-        exponentiate(0)
         transpose_h(3)
         load_h(H_BUFS + 1)
-        interleave_w("ca")
-        weigh_b(0)
-        quantize_w("ca")
         project(0, "ca")
+        exponentiate(0)
+        sort_h(5)
         quantize_h(3)
+        weigh_b(0)
         weigh_a(0)
         sum4(0)
 
         last = GROUPS - 1
-        for g in range(1, GROUPS):
-            ahead = g < last
-            if g >= 2:
-                emit(g - 2)
-            if ahead:
-                transpose_h(2 * g + 2)
-                if 2 * g + H_BUFS < 2 * GROUPS:
-                    load_h(2 * g + H_BUFS)
+        for g in range(1, last):
+            transpose_h(2 * g + 2)
+            if 2 * g + H_BUFS < 2 * GROUPS:
+                load_h(2 * g + H_BUFS)
+            quantize_h(2 * g + 2, 0, 1)
             project(g, "zb")
             project(g, "za")
-            add_bias(g, "zb")
-            add_bias(g, "za")
-            if ahead:
-                quantize_h(2 * g + 2)
-                transpose_h(2 * g + 3)
-                if 2 * g + H_BUFS + 1 < 2 * GROUPS:
-                    load_h(2 * g + H_BUFS + 1)
-            sum2(g - 1)
-            max4(g)
-            sum1(g - 1)
-            max2(g)
-            invert(g - 1)
-            max1(g)
-            normalise(g - 1)
+            add_bias(g)
+            if g + 2 < GROUPS:
+                sort_h(2 * g + 4)
+            if g >= 2:
+                emit(g - 2)
+            transpose_h(2 * g + 3)
+            if 2 * g + H_BUFS + 1 < 2 * GROUPS:
+                load_h(2 * g + H_BUFS + 1)
+            if g + 2 < GROUPS:
+                sort_h(2 * g + 5)
             project(g, "cb")
             project(g, "ca")
-            if ahead:
-                shift(g)
-                exponentiate(g)
-                quantize_h(2 * g + 3)
-                weigh_b(g)
-                weigh_a(g)
+            sum2(g - 1)
+            max4(g, 0, 2)
+            sum1(g - 1)
+            max4(g, 2, 4)
+            pair_products(g - 1)
+            quantize_h(2 * g + 2, 1, 2)
+            quad_products(g - 1)
+            max2(g)
+            invert_quads(g - 1)
+            max1(g)
+            quantize_h(2 * g + 3, 0, 1 if g < last - 1 else 2)
+            invert_pairs(g - 1)
+            shift_b(g)
+            exponentiate(g, 0, M)
+            invert(g - 1)
+            shift_a(g)
+            exponentiate(g, M, 2 * M)
+            normalise(g - 1)
+            if g < last - 1:
+                quantize_h(2 * g + 3, 1, 2)
+            weigh_b(g)
+            weigh_a(g)
+            if g < last - 1:
                 sum4(g)
 
-        emit(last - 1)
-        denominators = psum.tile([P, P], F32, name="acc_zb")
-        numerators = psum.tile([P, P], F32, name="acc_za")
-        shift(last, 0, M)
+        def turned_sums(g):
+            banks = [psum.tile([P, P], F32, name="turned", bufs=4) for s in range(2)]
+            for s in range(2):
+                sum_turned(g, s, banks[s], 0, 2 * M)
+            return banks
+
+        def invert_turned(inverse, denominators, cols):
+            nc.vector.reciprocal(out=inverse[:, cols], in_=denominators[:, cols])
+
+        def emit_turned(g, numerators, inverse):
+            rows = stream.tile([P, HD], F32, name="rows")
+            nc.vector.tensor_tensor(out=rows[:], in0=numerators[:], in1=inverse[:], op=ALU.mult)
+            nc.sync.dma_start(out=out_rows[g * P : (g + 1) * P, :], in_=rows[:])
+
+        project(last, "zb")
+        project(last, "za")
+        add_bias(last)
+        denominators, numerators = turned_sums(last - 1)
+        emit(last - 2, "turned", 4)
+        project(last, "cb")
+        project(last, "ca")
+        inverse = stream.tile([P, P], F32, name="inverse")
+        max4(last, 0, M)
+        invert_turned(inverse, denominators, slice(0, HD // 2))
+        max2(last)
+        invert_turned(inverse, denominators, slice(HD // 2, HD))
+        max1(last)
+        emit_turned(last - 1, numerators, inverse)
+        shift_b(last)
         exponentiate(last, 0, M)
-        shift(last, M, 2 * M)
+        shift_a(last)
         exponentiate(last, M, 2 * M)
         weigh_b(last)
         weigh_a(last)
-        sum_turned(last, 0, denominators, 0, 2 * M)
-        sum_turned(last, 1, numerators, 0, 2 * M)
+        denominators, numerators = turned_sums(last)
         inverse = stream.tile([P, P], F32, name="inverse")
-        nc.vector.reciprocal(out=inverse[:], in_=denominators[:])
-        rows = stream.tile([P, HD], F32, name="rows")
-        nc.vector.tensor_tensor(out=rows[:], in0=numerators[:], in1=inverse[:], op=ALU.mult)
-        nc.sync.dma_start(out=out_rows[last * P :, :], in_=rows[:])
+        invert_turned(inverse, denominators, slice(0, HD))
+        emit_turned(last, numerators, inverse)

from contextlib import ExitStack

import concourse.mybir as mybir
from concourse.masks import make_identity

F32 = mybir.dt.float32
BF16 = mybir.dt.bfloat16
U32 = mybir.dt.uint32
U8 = mybir.dt.uint8
E4M3X4 = mybir.dt.float8_e4m3fn_x4
E5M2X4 = mybir.dt.float8_e5m2_x4
ALU = mybir.AluOpType
ACT = mybir.ActivationFunctionType

B, S, D, HD, M = 4, 1024, 2048, 128, 4
P = 128
K_PASS = 512
PASSES = D // K_PASS
TOK = P * M
GROUPS = B * S // TOK
BLOCKS = S // M
L_COLS = BLOCKS + 8
NEG = -(2.0 - 2.0 ** -23) * 2.0 ** 127
H_BUFS = 8
SORTED = (2, 2)

FLOPS = 2 * B * S * D * 4 * HD


def tile_tokenlevelcompressor_pa_kernel(tc, h, w_kv_a, w_kv_b, w_z_a, w_z_b, b_a, b_b, out):
    nc = tc.nc
    h_rows = h.flatten_outer_dims()
    out_rows = out.flatten_outer_dims()

    with ExitStack() as ctx:
        keep = ctx.enter_context(tc.tile_pool(name="keep", bufs=1))
        stream = ctx.enter_context(tc.tile_pool(name="stream", bufs=2))
        psum = ctx.enter_context(tc.psum_pool(name="psum", bufs=1))
        ctx.enter_context(tc.manual_schedule())

        ident = keep.tile([P, P], F32, name="ident")
        bias_rows = keep.tile([2 * M, HD], BF16, name="bias_rows")
        bias_sq = keep.tile([P, P], F32, name="bias_sq")
        bias = keep.tile([P, 2 * M], F32, name="bias")
        logits = [keep.tile([P, M, L_COLS], F32, name="logits%d" % s) for s in range(2)]
        terms = [keep.tile([P, 2, 2 * M, P], F32, name="terms%d" % s) for s in range(2)]
        carry = keep.tile([P, M, 1], F32, name="carry")
        weights = {"za": w_z_a, "zb": w_z_b, "ca": w_kv_a, "cb": w_kv_b}
        w_raw, w_codes, w_scales = {}, {}, {}
        for key in weights:
            w_raw[key] = keep.tile([P, PASSES, M, HD], BF16, name="w_raw_" + key)
            w_codes[key] = keep.tile([P, PASSES * HD], U32, name="w_codes_" + key, align_bytes=64)
            w_scales[key] = keep.tile([P, PASSES * HD], U8, name="w_scales_" + key, align_bytes=64)

        h_raw, h_sorted, h_side, h_codes, h_scales, acc, result = {}, {}, {}, {}, {}, {}, {}
        state = {}

        def load_h(n, first=0, last=2):
            g, half = divmod(n, 2)
            if first == 0:
                h_raw[n] = stream.tile([P, M, 2 * K_PASS], BF16, name="h_raw", bufs=H_BUFS)
            rows = h_rows[g * TOK : (g + 1) * TOK, half * 2 * K_PASS : (half + 1) * 2 * K_PASS]
            cols = slice(first * K_PASS, last * K_PASS)
            nc.sync.dma_start(out=h_raw[n][:, :, cols], in_=rows.rearrange("(j i) k -> j i k", i=M)[:, :, cols])

        def load_w(key):
            nc.sync.dma_start(out=w_raw[key][:], in_=weights[key].rearrange("(g p t) c -> p g t c", p=P, t=4))

        def interleave_w(key, copy=nc.vector.tensor_copy):
            side = stream.tile([P, PASSES, HD, 4], BF16, name="w_side", align_bytes=64)
            for g in range(PASSES):
                copy(
                    out=side[:, g].rearrange("p (c i) t -> p c t i", i=4),
                    in_=w_raw[key][:, g].rearrange("p t (c i) -> p c t i", i=4),
                )
            state["side", key] = side

        def quantize_w(key):
            nc.vector.quantize_mx(
                out=w_codes[key][:].bitcast(E4M3X4),
                scales=w_scales[key][:],
                in_=state["side", key][:].rearrange("p g c t -> p (g c t)"),
            )

        def sort_h(n):
            count = SORTED[n % 2]
            if count == 0:
                return
            words = h_raw[n][:].rearrange("p i k -> p (i k)").bitcast(F32).rearrange("p (i w) -> p i w", i=M)
            h_sorted[n] = stream.tile([P, M, 2, P], F32, name="h_sorted", bufs=3)
            first = M - 2 * count
            nc.scalar.copy(
                out=h_sorted[n][:, first:],
                in_=words[:, first:, 256:512].rearrange("p i (r u) -> p i u r", u=2),
            )

        def transpose_h(n, first=0, last=2):
            words = h_raw[n][:].rearrange("p i k -> p (i k)").bitcast(F32)
            if first == 0:
                h_side[n] = stream.tile([P, 2 * TOK * 4], BF16, name="h_side", bufs=3, align_bytes=64)
            side_words = h_side[n][:].bitcast(F32)
            for q in range(first, last):
                for pair in range(2):
                    bank = psum.tile([P, 2, 2, P], F32, name="turned", bufs=4)
                    for ii in range(2):
                        base = (2 * pair + ii) * K_PASS + q * 256
                        for u in range(2):
                            if n in h_sorted and q == 1 and pair >= 2 - SORTED[n % 2]:
                                source = h_sorted[n][:, 2 * pair + ii, u, :]
                            else:
                                source = words[:, base + u : base + 256 : 2]
                            nc.tensor.transpose(bank[:, ii, u, :], source, ident[:])
                    at = q * 1024 + pair * 512
                    nc.scalar.copy(
                        out=side_words[:, at : at + 512].rearrange("p (i r u) -> p i r u", i=2, u=2),
                        in_=bank[:].rearrange("p i u r -> p i r u"),
                    )

        def quantize_h(n, first=0, last=2):
            if first == 0:
                h_codes[n] = stream.tile([P, 2 * TOK], U32, name="h_codes", bufs=4, align_bytes=64)
                h_scales[n] = stream.tile([P, 2 * TOK], U8, name="h_scales", bufs=4, align_bytes=64)
            cols = slice(first * TOK, last * TOK)
            nc.vector.quantize_mx(
                out=h_codes[n][:, cols].bitcast(E5M2X4),
                scales=h_scales[n][:, cols],
                in_=h_side[n][:, first * TOK * 4 : last * TOK * 4],
            )

        def project(g, key, first=0, last=PASSES):
            if first == 0:
                acc[key] = psum.tile([P, M, P], F32, name="acc_" + key)
            for k in range(first, last):
                n, q = 2 * g + k // 2, k % 2
                w_cols = slice(k * HD, (k + 1) * HD)
                h_cols = slice(q * TOK, (q + 1) * TOK)
                nc.tensor.matmul_mx(
                    out=acc[key][:].rearrange("p i j -> p (i j)"),
                    lhsT=w_codes[key][:, w_cols].bitcast(E4M3X4),
                    lhsT_scale=w_scales[key][:, w_cols],
                    rhs=h_codes[n][:, h_cols].bitcast(E5M2X4),
                    rhs_scale=h_scales[n][:, h_cols],
                    start=(k == 0),
                    stop=(k == PASSES - 1),
                )

        def add_bias(g):
            seq, half = divmod(g, 2)
            for i in range(M):
                nc.scalar.activation(
                    out=logits[seq % 2][:, i, half * P + 1 : (half + 1) * P + 1],
                    in_=acc["zb"][:, i, :],
                    func=ACT.Identity,
                    bias=bias[:, i : i + 1],
                )

        def window(g):
            seq, half = divmod(g, 2)
            return logits[seq % 2][:, :, half * P : (half + 1) * P]

        def max4(g, first, last):
            if first == 0:
                state["max4"] = stream.tile([P, M, P], F32, name="max4")
            for i in range(first, last):
                nc.vector.scalar_tensor_tensor(
                    out=state["max4"][:, i, :],
                    in0=acc["za"][:, i, :],
                    scalar=bias[:, M + i : M + i + 1],
                    in1=window(g)[:, i, :],
                    op0=ALU.add,
                    op1=ALU.max,
                )

        def max2(g):
            t = stream.tile([P, 2, P], F32, name="max2")
            nc.vector.tensor_tensor(out=t[:], in0=state["max4"][:, 0:2, :], in1=state["max4"][:, 2:4, :], op=ALU.max)
            state["max2"] = t

        def max1(g):
            t = stream.tile([P, 1, P], F32, name="max1")
            nc.vector.tensor_tensor(out=t[:], in0=state["max2"][:, 0:1, :], in1=state["max2"][:, 1:2, :], op=ALU.max)
            state["max1"] = t

        def shift_b(g):
            state["shifted"] = stream.tile([P, 2 * M, P], F32, name="shifted")
            nc.vector.tensor_tensor(
                out=state["shifted"][:, 0:M, :],
                in0=window(g),
                in1=state["max1"][:].to_broadcast([P, M, P]),
                op=ALU.subtract,
            )

        def shift_a(g):
            for i in range(M):
                nc.vector.scalar_tensor_tensor(
                    out=state["shifted"][:, M + i, :],
                    in0=acc["za"][:, i, :],
                    scalar=bias[:, M + i : M + i + 1],
                    in1=state["max1"][:, 0, :],
                    op0=ALU.add,
                    op1=ALU.subtract,
                )

        def exponentiate(g, first=0, last=2 * M):
            nc.scalar.activation(
                out=terms[g % 2][:, 0, first:last, :], in_=state["shifted"][:, first:last, :], func=ACT.Exp
            )

        def weigh_b(g):
            t = terms[g % 2]
            nc.vector.tensor_tensor(
                out=t[:, 1, 0:M, 1:P], in0=acc["cb"][:, :, 0 : P - 1], in1=t[:, 0, 0:M, 1:P], op=ALU.mult
            )
            if g % 2 == 0:
                nc.vector.tensor_copy(out=carry[:], in_=acc["cb"][:, :, P - 1 : P])
            else:
                nc.vector.tensor_tensor(out=t[:, 1, 0:M, 0:1], in0=carry[:], in1=t[:, 0, 0:M, 0:1], op=ALU.mult)

        def weigh_a(g):
            t = terms[g % 2]
            nc.vector.tensor_tensor(out=t[:, 1, M:, :], in0=acc["ca"][:], in1=t[:, 0, M:, :], op=ALU.mult)

        def sum4(g):
            t = stream.tile([P, 2, 4, P], F32, name="sum4")
            for s in range(2):
                nc.vector.tensor_tensor(
                    out=t[:, s], in0=terms[g % 2][:, s, 0:4, :], in1=terms[g % 2][:, s, 4:8, :], op=ALU.add
                )
            state["sum4"] = t

        def sum2(g):
            t = stream.tile([P, 2, 2, P], F32, name="sum2")
            s4 = state["sum4"]
            nc.vector.tensor_tensor(out=t[:], in0=s4[:, :, 0:2, :], in1=s4[:, :, 2:4, :], op=ALU.add)
            state["sum2"] = t

        def sum1(g):
            t = stream.tile([P, 2, P], F32, name="sum1")
            s2 = state["sum2"]
            nc.vector.tensor_tensor(out=t[:], in0=s2[:, :, 0, :], in1=s2[:, :, 1, :], op=ALU.add)
            state["sum1"] = t

        def pair_products(g):
            t = stream.tile([P, 2, P // 4], F32, name="pairs")
            den = state["sum1"][:, 0, :]
            nc.vector.tensor_tensor(
                out=t[:].rearrange("p a j -> p (a j)"), in0=den[:, 0 : P // 2], in1=den[:, P // 2 :], op=ALU.mult
            )
            state["pairs"] = t

        def quad_products(g):
            t = stream.tile([P, 1, P // 4], F32, name="quads")
            nc.vector.tensor_tensor(out=t[:], in0=state["pairs"][:, 0:1, :], in1=state["pairs"][:, 1:2, :], op=ALU.mult)
            state["quads"] = t

        def invert_quads(g):
            t = stream.tile([P, 1, P // 4], F32, name="quad_inverse")
            nc.vector.reciprocal(out=t[:], in_=state["quads"][:])
            state["quad_inverse"] = t

        def invert_pairs(g):
            t = stream.tile([P, 1, P // 2], F32, name="pair_inverse")
            nc.vector.tensor_tensor(
                out=t[:].rearrange("p o (a j) -> p (o a) j", a=2),
                in0=state["pairs"][:, ::-1, :],
                in1=state["quad_inverse"][:].to_broadcast([P, 2, P // 4]),
                op=ALU.mult,
            )
            state["pair_inverse"] = t

        def invert(g):
            t = stream.tile([P, P], F32, name="inverse")
            nc.vector.tensor_tensor(
                out=t[:].rearrange("p (a j) -> p a j", a=2),
                in0=state["sum1"][:, 0, :].rearrange("p (a j) -> p a j", a=2)[:, ::-1, :],
                in1=state["pair_inverse"][:].to_broadcast([P, 2, P // 2]),
                op=ALU.mult,
            )
            state["inverse"] = t

        def normalise(g):
            result[g] = stream.tile([P, P], F32, name="result")
            nc.vector.tensor_tensor(out=result[g][:], in0=state["sum1"][:, 1, :], in1=state["inverse"][:], op=ALU.mult)

        def emit(g, tag="acc_cb", bufs=1):
            bank = psum.tile([P, P], F32, name=tag, bufs=bufs)
            nc.tensor.transpose(bank[:], result[g][:], ident[:])
            rows = stream.tile([P, HD], F32, name="rows")
            nc.scalar.copy(out=rows[:], in_=bank[:])
            nc.sync.dma_start(out=out_rows[g * P : (g + 1) * P, :], in_=rows[:])

        def sum_turned(g, s, bank, first, last):
            for e in range(first, last):
                nc.tensor.matmul(
                    out=bank[:],
                    lhsT=terms[g % 2][:, s, e, :],
                    rhs=ident[:],
                    start=(e == 0),
                    stop=(e == 2 * M - 1),
                    is_transpose=True,
                )

        nc.scalar.dma_start(out=bias_rows[0:M, :], in_=b_b)
        nc.scalar.dma_start(out=bias_rows[M : 2 * M, :], in_=b_a)
        load_h(0, 0, 1)
        load_w("zb")
        load_h(0, 1, 2)
        load_w("za")
        load_h(1, 0, 1)
        load_h(1, 1, 2)
        load_h(2)
        load_w("cb")
        load_h(3)
        load_w("ca")
        for n in range(4, H_BUFS):
            load_h(n)
        make_identity(nc, ident[:])
        nc.gpsimd.memset(bias_sq[:], 0.0)
        for s in range(2):
            nc.vector.memset(logits[s][:, 0:M, 0:1], NEG)
        nc.vector.memset(terms[0][:, 1, 0:M, 0:1], 0.0)
        nc.scalar.activation(out=bias_sq[0 : 2 * M, :], in_=bias_rows[:], func=ACT.Identity)

        transpose_h(0, 0, 1)
        bias_bank = psum.tile([P, P], F32, name="acc_ca")
        nc.tensor.transpose(bias_bank[:], bias_sq[:], ident[:])
        nc.scalar.copy(out=bias[:], in_=bias_bank[:, 0 : 2 * M])
        interleave_w("zb")
        quantize_h(0, 0, 1)
        quantize_w("zb")
        transpose_h(0, 1, 2)
        interleave_w("za")
        quantize_h(0, 1, 2)
        quantize_w("za")
        transpose_h(1, 0, 1)
        quantize_h(1, 0, 1)
        project(0, "zb", 0, 1)
        project(0, "za", 0, 1)
        transpose_h(1, 1, 2)
        quantize_h(1, 1, 2)
        project(0, "zb", 1, 2)
        project(0, "za", 1, 2)
        project(0, "zb", 2, 3)
        project(0, "za", 2, 3)
        project(0, "zb", 3, 4)
        project(0, "za", 3, 4)
        add_bias(0)
        transpose_h(2)
        load_h(H_BUFS)
        interleave_w("cb")
        max4(0, 0, M)
        quantize_w("cb")
        max2(0)
        project(0, "cb")
        max1(0)
        interleave_w("ca")
        shift_b(0)
        shift_a(0)
        quantize_w("ca")
        quantize_h(2)
        transpose_h(3)
        load_h(H_BUFS + 1)
        project(0, "ca")
        exponentiate(0)
        sort_h(5)
        quantize_h(3)
        weigh_b(0)
        weigh_a(0)
        sum4(0)

        last = GROUPS - 1
        for g in range(1, last):
            transpose_h(2 * g + 2)
            if 2 * g + H_BUFS < 2 * GROUPS:
                load_h(2 * g + H_BUFS)
            quantize_h(2 * g + 2, 0, 1)
            project(g, "zb")
            project(g, "za")
            add_bias(g)
            if g + 2 < GROUPS:
                sort_h(2 * g + 4)
            if g >= 2:
                emit(g - 2)
            transpose_h(2 * g + 3)
            if 2 * g + H_BUFS + 1 < 2 * GROUPS:
                load_h(2 * g + H_BUFS + 1)
            if g + 2 < GROUPS:
                sort_h(2 * g + 5)
            project(g, "cb")
            project(g, "ca")
            sum2(g - 1)
            max4(g, 0, 2)
            sum1(g - 1)
            max4(g, 2, 4)
            pair_products(g - 1)
            quantize_h(2 * g + 2, 1, 2)
            quad_products(g - 1)
            max2(g)
            invert_quads(g - 1)
            max1(g)
            quantize_h(2 * g + 3, 0, 1 if g < last - 1 else 2)
            invert_pairs(g - 1)
            shift_b(g)
            exponentiate(g, 0, M)
            invert(g - 1)
            shift_a(g)
            exponentiate(g, M, 2 * M)
            normalise(g - 1)
            if g < last - 1:
                quantize_h(2 * g + 3, 1, 2)
            weigh_b(g)
            weigh_a(g)
            if g < last - 1:
                sum4(g)

        def turned_sums(g):
            banks = [psum.tile([P, P], F32, name="turned", bufs=4) for s in range(2)]
            for s in range(2):
                sum_turned(g, s, banks[s], 0, 2 * M)
            return banks

        def invert_turned(inverse, denominators, cols):
            nc.vector.reciprocal(out=inverse[:, cols], in_=denominators[:, cols])

        def emit_turned(g, numerators, inverse):
            rows = stream.tile([P, HD], F32, name="rows")
            nc.vector.tensor_tensor(out=rows[:], in0=numerators[:], in1=inverse[:], op=ALU.mult)
            nc.sync.dma_start(out=out_rows[g * P : (g + 1) * P, :], in_=rows[:])

        project(last, "zb")
        project(last, "za")
        add_bias(last)
        denominators, numerators = turned_sums(last - 1)
        emit(last - 2, "turned", 4)
        project(last, "cb")
        project(last, "ca")
        inverse = stream.tile([P, P], F32, name="inverse")
        max4(last, 0, M)
        invert_turned(inverse, denominators, slice(0, HD // 2))
        max2(last)
        invert_turned(inverse, denominators, slice(HD // 2, HD))
        max1(last)
        emit_turned(last - 1, numerators, inverse)
        shift_b(last)
        exponentiate(last, 0, M)
        shift_a(last)
        exponentiate(last, M, 2 * M)
        weigh_b(last)
        weigh_a(last)
        denominators, numerators = turned_sums(last)
        inverse = stream.tile([P, P], F32, name="inverse")
        invert_turned(inverse, denominators, slice(0, HD))
        emit_turned(last, numerators, inverse)
